import numpy as np
import ml_dtypes


def mxq(x, axis, fmt="e4m3"):
    dtype, down = {"e4m3": (ml_dtypes.float8_e4m3fn, 7), "e5m2": (ml_dtypes.float8_e5m2, 14)}[fmt]
    v = np.moveaxis(np.asarray(x, np.float32).astype(ml_dtypes.bfloat16).astype(np.float64), axis, -1)
    blocks = v.reshape(v.shape[:-1] + (-1, 32))
    amax = np.abs(blocks).max(-1, keepdims=True)
    byte = np.maximum(np.where(amax > 0, np.frexp(amax)[1] - 1 + 127, 0) - down, 1)
    scale = np.exp2(byte - 127.0)
    codes = (blocks / scale).astype(np.float32).astype(dtype).astype(np.float64)
    return np.moveaxis((codes * scale).reshape(v.shape), -1, axis)


WIDE = False


def mx_kscale(k):
    if not WIDE:
        return np.ones(k)
    levels = np.array([10, -10, 5, -5, 0])
    a = np.random.permutation(np.resize(levels, k // 512 * 4)).reshape(k // 512, 4)
    idx = np.arange(k)
    return np.exp2(a[idx // 512, idx % 128 // 32])


BF16 = ml_dtypes.bfloat16


def bf(x):
    return np.asarray(x, np.float32).astype(BF16)


def f64(x):
    return np.asarray(x).astype(np.float64)


B, D, R = 8192, 1024, 128


def softplus(v):
    return np.log1p(np.exp(v))


def setup_inputs():
    s = mx_kscale(D)
    w = 1.0 / np.sqrt(D)
    return {"x": bf(np.random.standard_normal((B, D)) * s),
            "state_re": bf(np.random.standard_normal((B, R))),
            "state_im": bf(np.random.standard_normal((B, R))),
            "W_dt": bf(np.random.standard_normal((R, D)) * 0.5 * w / s),
            "b_dt": bf(np.random.standard_normal(R) * 0.3),
            "W_ph": bf(np.random.standard_normal((R, D)) * 0.5 * w / s),
            "b_ph": bf(np.random.standard_normal(R) * 0.3),
            "W_B": bf(np.random.standard_normal((R, D)) * w / s),
            "A_real": bf(np.random.standard_normal(R) * 0.5),
            "A_imag": bf(np.random.standard_normal(R) * 0.5)}


def reference(x, state_re, state_im, W_dt, b_dt, W_ph, b_ph, W_B, A_real, A_imag):
    xq = mxq(f64(x), 1, "e4m3")
    dt = softplus((xq @ mxq(f64(W_dt), 1, "e4m3").T) + f64(b_dt))
    phase = np.tanh((xq @ mxq(f64(W_ph), 1, "e4m3").T) + f64(b_ph)) * np.pi
    decay = np.exp(-dt * np.exp(f64(A_real)))
    angle = dt * f64(A_imag) + phase
    B_val = xq @ mxq(f64(W_B), 1, "e4m3").T
    cos = np.cos(angle)
    sin = np.sin(angle)
    new_re = (f64(state_re) * cos - f64(state_im) * sin) * decay + B_val
    new_im = (f64(state_re) * sin + f64(state_im) * cos) * decay
    return new_re, new_im

@@ -1,0 +1,332 @@
+import math
+from contextlib import ExitStack
+
+import concourse.mybir as mybir
+from concourse.masks import make_identity
+
+F32 = mybir.dt.float32
+BF16 = mybir.dt.bfloat16
+U32 = mybir.dt.uint32
+U8 = mybir.dt.uint8
+FP8X4 = mybir.dt.float8_e4m3fn_x4
+ACT = mybir.ActivationFunctionType
+ALU = mybir.AluOpType
+
+P = 128
+ROWS, K, CH = 8192, 1024, 128
+FLOPS = 2 * ROWS * K * 3 * CH
+TILES = ROWS // P
+GROUP_TILES = 4
+GROUP_ROWS = GROUP_TILES * P
+GROUPS = TILES // GROUP_TILES
+BATCH = 4
+BATCHES = GROUPS // BATCH
+PASSES = K // 512
+ROW_WORDS = K // 2
+UNIT = 256
+GROUP_UNITS = PASSES * GROUP_ROWS // UNIT
+STEP_UNITS = 2
+EXP_TANH, LOG, DECAY, SINES = 0, 1, 2, 3
+FINISH_LAG = 4
+PREFETCH = 2
+ROUND_MAGIC = 1.5 * 2.0**23
+FEED_BANKS = 5
+AHEAD = 2
+WEIGHTS = ("dt", "ph", "b")
+
+
+def tile_mamba3mimoblock_pa_t_kernel(
+    tc, x, state_re, state_im, W_dt, b_dt, W_ph, b_ph, W_B, A_real, A_imag, out_0, out_1
+):
+    nc = tc.nc
+    x_tiles = x.rearrange("(p t) k -> p t k", t=TILES)
+    re_tiles = state_re.rearrange("(p t) c -> p t c", t=TILES)
+    im_tiles = state_im.rearrange("(p t) c -> p t c", t=TILES)
+    new_re_tiles = out_0.rearrange("(p t) c -> p t c", t=TILES)
+    new_im_tiles = out_1.rearrange("(p t) c -> p t c", t=TILES)
+
+    with ExitStack() as stack:
+        stack.enter_context(tc.manual_schedule())
+        const = stack.enter_context(tc.tile_pool(name="const", bufs=1))
+        xin = stack.enter_context(tc.tile_pool(name="xin", bufs=PREFETCH + 1))
+        stage = stack.enter_context(tc.tile_pool(name="stage", bufs=3))
+        quant = stack.enter_context(tc.tile_pool(name="quant", bufs=3 * BATCH))
+        chan = stack.enter_context(tc.tile_pool(name="chan", bufs=BATCH))
+        rows = stack.enter_context(tc.tile_pool(name="rows", bufs=3))
+        psum = stack.enter_context(tc.psum_pool(name="psum", bufs=1))
+
+        def transpose_words(word_blocks):
+            planes = psum.tile([P, 2, UNIT], F32, name="planes", tag="feed", bufs=FEED_BANKS)
+            for j, pair in enumerate(word_blocks):
+                for u, words in enumerate(pair):
+                    nc.tensor.transpose(planes[:, u, j * P : (j + 1) * P], words, ident[:])
+            return planes
+
+        def copy_words(planes, grouped_cols, on_vector):
+            dst = grouped_cols.bitcast(F32).rearrange("p (r u) -> p r u", u=2)
+            src = planes[:].rearrange("p u r -> p r u")
+            if on_vector:
+                nc.vector.tensor_copy(out=dst, in_=src)
+            else:
+                nc.scalar.copy(out=dst, in_=src)
+
+        def quantise(grouped, codes_cols, scales_cols):
+            nc.vector.quantize_mx(out=codes_cols.bitcast(FP8X4), scales=scales_cols, in_=grouped)
+
+        vec_rows = const.tile([P, P], BF16, name="vec_rows")
+        nc.vector.memset(vec_rows[:], 0.0)
+        for j, vec in enumerate((b_dt, b_ph, A_real, A_imag)):
+            nc.sync.dma_start(out=vec_rows[j : j + 1, :], in_=vec.rearrange("(o c) -> o c", o=1))
+        w_raw = {}
+        for name, w in zip(WEIGHTS, (W_dt, W_ph, W_B)):
+            w_raw[name] = const.tile([P, K], BF16, name="w_raw_" + name)
+            nc.sync.dma_start(out=w_raw[name][:], in_=w)
+
+        x_raw = {}
+
+        def load_x(g):
+            x_raw[g] = xin.tile([P, GROUP_TILES * K], BF16, name="x_raw")
+            nc.sync.dma_start(
+                out=x_raw[g][:].rearrange("p (t k) -> p t k", t=GROUP_TILES),
+                in_=x_tiles[:, g * GROUP_TILES : (g + 1) * GROUP_TILES, :],
+            )
+
+        for g in range(PREFETCH):
+            load_x(g)
+
+        re_all = const.tile([P, TILES * CH], BF16, name="re_all")
+        im_all = const.tile([P, TILES * CH], BF16, name="im_all")
+
+        def load_state(batch):
+            t0, t1 = batch * BATCH * GROUP_TILES, (batch + 1) * BATCH * GROUP_TILES
+            for dst, src in ((re_all, re_tiles), (im_all, im_tiles)):
+                nc.sync.dma_start(
+                    out=dst[:, t0 * CH : t1 * CH].rearrange("p (t c) -> p t c", c=CH), in_=src[:, t0:t1, :]
+                )
+
+        ident = const.tile([P, P], F32, name="ident")
+        make_identity(nc, ident[:])
+
+        vec_f32 = const.tile([P, P], F32, name="vec_f32")
+        nc.vector.tensor_copy(out=vec_f32[:], in_=vec_rows[:])
+        planes = psum.tile([P, 2, UNIT], F32, name="planes", tag="feed", bufs=FEED_BANKS)
+        nc.tensor.transpose(planes[:, 0, 0:P], vec_f32[:], ident[:])
+        per_channel = const.tile([P, 4], F32, name="per_channel")
+        nc.vector.tensor_copy(out=per_channel[:], in_=planes[:, 0, 0:4])
+        bias_dt, bias_ph = per_channel[:, 0:1], per_channel[:, 1:2]
+        rate = const.tile([P, 1], F32, name="rate")
+        nc.scalar.activation(out=rate[:], in_=per_channel[:, 2:3], func=ACT.Exp)
+        neg_rate = const.tile([P, 1], F32, name="neg_rate")
+        nc.vector.tensor_scalar(out=neg_rate[:], in0=rate[:], scalar1=-1.0, scalar2=None, op0=ALU.mult)
+        half_turns = const.tile([P, 1], F32, name="half_turns")
+        nc.vector.tensor_scalar(
+            out=half_turns[:], in0=per_channel[:, 3:4], scalar1=1.0 / math.pi, scalar2=None, op0=ALU.mult
+        )
+
+        w_codes = const.tile([P, len(WEIGHTS) * UNIT], U32, name="w_codes", align_bytes=64)
+        w_scales = const.tile([P, len(WEIGHTS) * UNIT], U8, name="w_scales", align_bytes=64)
+        for i, name in enumerate(WEIGHTS):
+            words = w_raw[name][:].bitcast(F32)
+            planes = transpose_words(
+                [[words[:, (2 * c + u) * P : (2 * c + u + 1) * P] for u in range(2)] for c in range(PASSES)]
+            )
+            grouped = stage.tile([P, 4 * UNIT], BF16, name="w_grouped", align_bytes=64, bufs=2)
+            copy_words(planes, grouped[:], on_vector=True)
+            quantise(grouped[:], w_codes[:, i * UNIT : (i + 1) * UNIT], w_scales[:, i * UNIT : (i + 1) * UNIT])
+
+        def weight(name, c):
+            lo = WEIGHTS.index(name) * UNIT + c * CH
+            return w_codes[:, lo : lo + CH].bitcast(FP8X4), w_scales[:, lo : lo + CH]
+
+        unit_planes, codes, scales = {}, {}, {}
+        step, angle, decay, cos_sin = {}, {}, {}, {}
+        turned, result, sums = {}, {}, {}
+
+        def transpose_unit(k):
+            g, in_group = divmod(k, GROUP_UNITS)
+            c, h = divmod(in_group, GROUP_ROWS // UNIT)
+            if in_group == 0 and g + PREFETCH < GROUPS:
+                load_x(g + PREFETCH)
+            words = x_raw[g][:].bitcast(F32)
+            blocks = []
+            for j in range(UNIT // P):
+                lo = (h * (UNIT // P) + j) * ROW_WORDS + 2 * c * P
+                blocks.append([words[:, lo + u * P : lo + (u + 1) * P] for u in range(2)])
+            unit_planes[k] = transpose_words(blocks)
+
+        def quantise_pass(grouped, g, c):
+            if c == 0:
+                codes[g] = quant.tile([P, PASSES * GROUP_ROWS], U32, name="codes", align_bytes=64)
+                scales[g] = quant.tile([P, PASSES * GROUP_ROWS], U8, name="scales", align_bytes=64)
+            cols = slice(c * GROUP_ROWS, (c + 1) * GROUP_ROWS)
+            quantise(grouped[:], codes[g][:, cols], scales[g][:, cols])
+
+        def multiply(g):
+            sums[g] = {}
+            for name in ("dt", "ph"):
+                sums[g][name] = psum.tile([P, GROUP_ROWS], F32, name="sums_" + name, tag="feed", bufs=FEED_BANKS)
+                for c in range(PASSES):
+                    w_c, w_s = weight(name, c)
+                    nc.tensor.matmul_mx(
+                        out=sums[g][name][:],
+                        lhsT=w_c,
+                        lhsT_scale=w_s,
+                        rhs=codes[g][:, c * GROUP_ROWS : (c + 1) * GROUP_ROWS].bitcast(FP8X4),
+                        rhs_scale=scales[g][:, c * GROUP_ROWS : (c + 1) * GROUP_ROWS],
+                        start=(c == 0),
+                        stop=(c == PASSES - 1),
+                    )
+
+        def exp_tanh(g):
+            step[g] = chan.tile([P, GROUP_ROWS], F32, name="step")
+            angle[g] = chan.tile([P, GROUP_ROWS], F32, name="angle")
+            nc.scalar.activation(out=step[g][:], in_=sums[g]["dt"][:], func=ACT.Exp, bias=bias_dt)
+            nc.scalar.activation(out=angle[g][:], in_=sums[g]["ph"][:], func=ACT.Tanh, bias=bias_ph)
+
+        def log(g):
+            nc.scalar.activation(out=step[g][:], in_=step[g][:], func=ACT.Ln, bias=1.0)
+
+        def wrap_angles(pair):
+            turns = {}
+            for g in pair:
+                turns[g] = chan.tile([P, GROUP_ROWS], F32, name="turns", bufs=2)
+                nc.vector.scalar_tensor_tensor(
+                    out=angle[g][:], in0=step[g][:], scalar=half_turns[:], in1=angle[g][:], op0=ALU.mult, op1=ALU.add
+                )
+            for g in pair:
+                nc.vector.tensor_scalar(
+                    out=turns[g][:], in0=angle[g][:], scalar1=0.5, scalar2=ROUND_MAGIC, op0=ALU.mult, op1=ALU.add
+                )
+            for g in pair:
+                nc.vector.tensor_scalar(
+                    out=turns[g][:], in0=turns[g][:], scalar1=ROUND_MAGIC, scalar2=2.0, op0=ALU.subtract, op1=ALU.mult
+                )
+            for g in pair:
+                nc.vector.tensor_tensor(out=angle[g][:], in0=angle[g][:], in1=turns[g][:], op=ALU.subtract)
+
+        def exp_decay(g):
+            decay[g] = chan.tile([P, GROUP_ROWS], F32, name="decay", bufs=BATCH + 2)
+            nc.scalar.activation(out=decay[g][:], in_=step[g][:], func=ACT.Exp, scale=neg_rate[:])
+
+        def sines(g):
+            cos_sin[g] = chan.tile([P, 2, GROUP_ROWS], F32, name="cos_sin", bufs=BATCH + 2)
+            nc.scalar.activation(out=cos_sin[g][:, 0, :], in_=angle[g][:], func=ACT.Abs)
+            nc.scalar.activation(out=cos_sin[g][:, 1, :], in_=angle[g][:], func=ACT.Sin, scale=math.pi)
+            nc.scalar.activation(
+                out=cos_sin[g][:, 0, :], in_=cos_sin[g][:, 0, :], func=ACT.Sin, scale=-math.pi, bias=math.pi / 2
+            )
+
+        def damp(g):
+            nc.vector.tensor_tensor(
+                out=cos_sin[g][:],
+                in0=cos_sin[g][:],
+                in1=decay[g][:].unsqueeze(1).to_broadcast([P, 2, GROUP_ROWS]),
+                op=ALU.mult,
+            )
+
+        def turn_to_rows(g):
+            cos_t = psum.tile([P, GROUP_ROWS], F32, name="cos_t")
+            sin_t = psum.tile([P, GROUP_ROWS], F32, name="sin_t")
+            drive = psum.tile([P, GROUP_ROWS], F32, name="drive")
+            for half, bank in enumerate((cos_t, sin_t)):
+                for i in range(GROUP_TILES):
+                    cols = slice(i * P, (i + 1) * P)
+                    nc.tensor.transpose(bank[:, cols], cos_sin[g][:, half, cols], ident[:])
+            for i in range(GROUP_TILES):
+                for c in range(PASSES):
+                    w_c, w_s = weight("b", c)
+                    lo = c * GROUP_ROWS + i * P
+                    nc.tensor.matmul_mx(
+                        out=drive[:, i * P : (i + 1) * P],
+                        lhsT=codes[g][:, lo : lo + P].bitcast(FP8X4),
+                        lhsT_scale=scales[g][:, lo : lo + P],
+                        rhs=w_c,
+                        rhs_scale=w_s,
+                        start=(c == 0),
+                        stop=(c == PASSES - 1),
+                    )
+            turned[g] = (cos_t, sin_t, drive)
+
+        def rotate_products(g):
+            cos_t, sin_t, drive = turned[g]
+            re = re_all[:, g * GROUP_ROWS : (g + 1) * GROUP_ROWS]
+            im = im_all[:, g * GROUP_ROWS : (g + 1) * GROUP_ROWS]
+            new_re = rows.tile([P, GROUP_ROWS], F32, name="new_re")
+            new_im = rows.tile([P, GROUP_ROWS], F32, name="new_im")
+            im_sin = rows.tile([P, GROUP_ROWS], F32, name="im_sin")
+            im_cos = rows.tile([P, GROUP_ROWS], F32, name="im_cos")
+            nc.vector.tensor_tensor(out=new_re[:], in0=re, in1=cos_t[:], op=ALU.mult)
+            nc.vector.tensor_tensor(out=im_cos[:], in0=im, in1=cos_t[:], op=ALU.mult)
+            nc.vector.tensor_tensor(out=new_im[:], in0=re, in1=sin_t[:], op=ALU.mult)
+            nc.vector.tensor_tensor(out=im_sin[:], in0=im, in1=sin_t[:], op=ALU.mult)
+            nc.vector.tensor_tensor(out=new_re[:], in0=new_re[:], in1=drive[:], op=ALU.add)
+            result[g] = (new_re, new_im, im_sin, im_cos)
+
+        def rotate_sums(g):
+            new_re, new_im, im_sin, im_cos = result[g]
+            nc.vector.tensor_tensor(out=new_im[:], in0=new_im[:], in1=im_cos[:], op=ALU.add)
+            nc.vector.tensor_tensor(out=new_re[:], in0=new_re[:], in1=im_sin[:], op=ALU.subtract)
+            tiles = slice(g * GROUP_TILES, (g + 1) * GROUP_TILES)
+            nc.sync.dma_start(out=new_im_tiles[:, tiles, :], in_=new_im[:].rearrange("p (t c) -> p t c", c=CH))
+            nc.sync.dma_start(out=new_re_tiles[:, tiles, :], in_=new_re[:].rearrange("p (t c) -> p t c", c=CH))
+
+        ROUND_ITEMS = 3 * BATCH
+
+        def prepare(item):
+            batch, j = divmod(item, ROUND_ITEMS)
+            if j < BATCH and 0 <= batch < BATCHES:
+                multiply(batch * BATCH + j)
+            if j >= BATCH and batch + 1 < BATCHES:
+                first = (batch + 1) * BATCH * GROUP_UNITS + (j - BATCH) * STEP_UNITS
+                for k in range(first, first + STEP_UNITS):
+                    transpose_unit(k)
+
+        for item in range(AHEAD):
+            prepare(-ROUND_ITEMS + LOG * BATCH + item)
+        copied = None
+        for phase in range(LOG - BATCH, GROUPS + FINISH_LAG):
+            batch, kind = divmod(phase, BATCH)
+            finishing = phase - FINISH_LAG
+            for q in range(BATCH):
+                g = batch * BATCH + q
+
+                if q == 0 and 0 <= finishing:
+                    rotate_products(finishing)
+                if q == 1 and 0 <= finishing + 1 < GROUPS:
+                    damp(finishing + 1)
+                    turn_to_rows(finishing + 1)
+                if q == 2 and 0 <= finishing:
+                    rotate_sums(finishing)
+
+                if copied is not None:
+                    quantise_pass(*copied)
+                copied = None
+                if kind in (LOG, DECAY) and batch + 1 < BATCHES:
+                    first = (batch + 1) * BATCH * GROUP_UNITS + ((kind - LOG) * BATCH + q) * STEP_UNITS
+                    grouped = stage.tile([P, 4 * GROUP_ROWS], BF16, name="grouped", align_bytes=64)
+                    for h in range(STEP_UNITS):
+                        copy_words(
+                            unit_planes[first + h],
+                            grouped[:, h * 4 * UNIT : (h + 1) * 4 * UNIT],
+                            on_vector=(batch < 1 and h == 0),
+                        )
+                    copied = (grouped, first // GROUP_UNITS, first % GROUP_UNITS // STEP_UNITS)
+                    if kind == DECAY and q == 0:
+                        load_state(batch + 1)
+
+                if 0 <= phase < GROUPS:
+                    if kind == EXP_TANH:
+                        exp_tanh(g)
+                    if kind == LOG:
+                        log(g)
+                        if q == 2:
+                            wrap_angles((g - 2, g - 1))
+                    if kind == DECAY:
+                        if q == 0:
+                            wrap_angles((g + 2, g + 3))
+                        exp_decay(g)
+                    if kind == SINES:
+                        sines(g)
+
+                if kind != SINES:
+                    prepare(batch * ROUND_ITEMS + kind * BATCH + q + AHEAD)

@@ -27,11 +27,15 @@ UNIT = 256
 GROUP_UNITS = PASSES * GROUP_ROWS // UNIT
 STEP_UNITS = 2
 EXP_TANH, LOG, DECAY, SINES = 0, 1, 2, 3
-FINISH_LAG = 4
 PREFETCH = 2
 ROUND_MAGIC = 1.5 * 2.0**23
 FEED_BANKS = 5
 AHEAD = 2
+QUANT_LAG = 2
+FINISH_STEPS = 8
+QUICK, SLOW = 3, 1
+FIRST_STEP = (-2 * FINISH_STEPS + 5) - QUICK
+IN_FLIGHT = BATCH + 3
 WEIGHTS = ("dt", "ph", "b")
 
 
@@ -49,8 +53,8 @@ def tile_mamba3mimoblock_pa_t_kernel(
         stack.enter_context(tc.manual_schedule())
         const = stack.enter_context(tc.tile_pool(name="const", bufs=1))
         xin = stack.enter_context(tc.tile_pool(name="xin", bufs=PREFETCH + 1))
-        stage = stack.enter_context(tc.tile_pool(name="stage", bufs=3))
-        quant = stack.enter_context(tc.tile_pool(name="quant", bufs=3 * BATCH))
+        stage = stack.enter_context(tc.tile_pool(name="stage", bufs=QUANT_LAG + 2))
+        quant = stack.enter_context(tc.tile_pool(name="quant", bufs=3 * BATCH + 1))
         chan = stack.enter_context(tc.tile_pool(name="chan", bufs=BATCH))
         rows = stack.enter_context(tc.tile_pool(name="rows", bufs=3))
         psum = stack.enter_context(tc.psum_pool(name="psum", bufs=1))
@@ -77,10 +81,9 @@ def tile_mamba3mimoblock_pa_t_kernel(
         nc.vector.memset(vec_rows[:], 0.0)
         for j, vec in enumerate((b_dt, b_ph, A_real, A_imag)):
             nc.sync.dma_start(out=vec_rows[j : j + 1, :], in_=vec.rearrange("(o c) -> o c", o=1))
-        w_raw = {}
-        for name, w in zip(WEIGHTS, (W_dt, W_ph, W_B)):
-            w_raw[name] = const.tile([P, K], BF16, name="w_raw_" + name)
-            nc.sync.dma_start(out=w_raw[name][:], in_=w)
+        w_raw = xin.tile([P, len(WEIGHTS) * K], BF16, name="w_raw", tag="x_raw")
+        for i, w in enumerate((W_dt, W_ph, W_B)):
+            nc.sync.dma_start(out=w_raw[:, i * K : (i + 1) * K], in_=w)
 
         x_raw = {}
 
@@ -126,11 +129,11 @@ def tile_mamba3mimoblock_pa_t_kernel(
         w_codes = const.tile([P, len(WEIGHTS) * UNIT], U32, name="w_codes", align_bytes=64)
         w_scales = const.tile([P, len(WEIGHTS) * UNIT], U8, name="w_scales", align_bytes=64)
         for i, name in enumerate(WEIGHTS):
-            words = w_raw[name][:].bitcast(F32)
+            words = w_raw[:, i * K : (i + 1) * K].bitcast(F32)
             planes = transpose_words(
                 [[words[:, (2 * c + u) * P : (2 * c + u + 1) * P] for u in range(2)] for c in range(PASSES)]
             )
-            grouped = stage.tile([P, 4 * UNIT], BF16, name="w_grouped", align_bytes=64, bufs=2)
+            grouped = stage.tile([P, 4 * UNIT], BF16, name="w_grouped", tag="grouped", align_bytes=64)
             copy_words(planes, grouped[:], on_vector=True)
             quantise(grouped[:], w_codes[:, i * UNIT : (i + 1) * UNIT], w_scales[:, i * UNIT : (i + 1) * UNIT])
 
@@ -205,11 +208,11 @@ def tile_mamba3mimoblock_pa_t_kernel(
                 nc.vector.tensor_tensor(out=angle[g][:], in0=angle[g][:], in1=turns[g][:], op=ALU.subtract)
 
         def exp_decay(g):
-            decay[g] = chan.tile([P, GROUP_ROWS], F32, name="decay", bufs=BATCH + 2)
+            decay[g] = chan.tile([P, GROUP_ROWS], F32, name="decay", bufs=IN_FLIGHT)
             nc.scalar.activation(out=decay[g][:], in_=step[g][:], func=ACT.Exp, scale=neg_rate[:])
 
         def sines(g):
-            cos_sin[g] = chan.tile([P, 2, GROUP_ROWS], F32, name="cos_sin", bufs=BATCH + 2)
+            cos_sin[g] = chan.tile([P, 2, GROUP_ROWS], F32, name="cos_sin", bufs=IN_FLIGHT)
             nc.scalar.activation(out=cos_sin[g][:, 0, :], in_=angle[g][:], func=ACT.Abs)
             nc.scalar.activation(out=cos_sin[g][:, 1, :], in_=angle[g][:], func=ACT.Sin, scale=math.pi)
             nc.scalar.activation(
@@ -247,28 +250,40 @@ def tile_mamba3mimoblock_pa_t_kernel(
                     )
             turned[g] = (cos_t, sin_t, drive)
 
-        def rotate_products(g):
-            cos_t, sin_t, drive = turned[g]
+        def finish_step(g, i):
+            if i == 5:
+                if 0 <= g + 1 < GROUPS:
+                    turn_to_rows(g + 1)
+                if 0 <= g + 2 < GROUPS:
+                    damp(g + 2)
+            if g < 0 or i == 5:
+                return
+            if i == 0:
+                result[g] = {}
+                for name in ("new_re", "new_im", "im_sin", "im_cos"):
+                    result[g][name] = rows.tile([P, GROUP_ROWS], F32, name=name)
             re = re_all[:, g * GROUP_ROWS : (g + 1) * GROUP_ROWS]
             im = im_all[:, g * GROUP_ROWS : (g + 1) * GROUP_ROWS]
-            new_re = rows.tile([P, GROUP_ROWS], F32, name="new_re")
-            new_im = rows.tile([P, GROUP_ROWS], F32, name="new_im")
-            im_sin = rows.tile([P, GROUP_ROWS], F32, name="im_sin")
-            im_cos = rows.tile([P, GROUP_ROWS], F32, name="im_cos")
-            nc.vector.tensor_tensor(out=new_re[:], in0=re, in1=cos_t[:], op=ALU.mult)
-            nc.vector.tensor_tensor(out=im_cos[:], in0=im, in1=cos_t[:], op=ALU.mult)
-            nc.vector.tensor_tensor(out=new_im[:], in0=re, in1=sin_t[:], op=ALU.mult)
-            nc.vector.tensor_tensor(out=im_sin[:], in0=im, in1=sin_t[:], op=ALU.mult)
-            nc.vector.tensor_tensor(out=new_re[:], in0=new_re[:], in1=drive[:], op=ALU.add)
-            result[g] = (new_re, new_im, im_sin, im_cos)
-
-        def rotate_sums(g):
-            new_re, new_im, im_sin, im_cos = result[g]
-            nc.vector.tensor_tensor(out=new_im[:], in0=new_im[:], in1=im_cos[:], op=ALU.add)
-            nc.vector.tensor_tensor(out=new_re[:], in0=new_re[:], in1=im_sin[:], op=ALU.subtract)
+            cos_t, sin_t, drive = turned[g]
+            new_re, new_im = result[g]["new_re"][:], result[g]["new_im"][:]
+            im_sin, im_cos = result[g]["im_sin"][:], result[g]["im_cos"][:]
             tiles = slice(g * GROUP_TILES, (g + 1) * GROUP_TILES)
-            nc.sync.dma_start(out=new_im_tiles[:, tiles, :], in_=new_im[:].rearrange("p (t c) -> p t c", c=CH))
-            nc.sync.dma_start(out=new_re_tiles[:, tiles, :], in_=new_re[:].rearrange("p (t c) -> p t c", c=CH))
+            if i == 0:
+                nc.vector.tensor_tensor(out=new_re, in0=re, in1=cos_t[:], op=ALU.mult)
+            if i == 1:
+                nc.vector.tensor_tensor(out=im_cos, in0=im, in1=cos_t[:], op=ALU.mult)
+            if i == 2:
+                nc.vector.tensor_tensor(out=new_im, in0=re, in1=sin_t[:], op=ALU.mult)
+            if i == 3:
+                nc.vector.tensor_tensor(out=im_sin, in0=im, in1=sin_t[:], op=ALU.mult)
+            if i == 4:
+                nc.vector.tensor_tensor(out=new_re, in0=new_re, in1=drive[:], op=ALU.add)
+            if i == 6:
+                nc.gpsimd.tensor_tensor(out=new_im, in0=new_im, in1=im_cos, op=ALU.add)
+                nc.sync.dma_start(out=new_im_tiles[:, tiles, :], in_=new_im.rearrange("p (t c) -> p t c", c=CH))
+            if i == 7:
+                nc.gpsimd.tensor_tensor(out=new_re, in0=new_re, in1=im_sin, op=ALU.subtract)
+                nc.sync.dma_start(out=new_re_tiles[:, tiles, :], in_=new_re.rearrange("p (t c) -> p t c", c=CH))
 
         ROUND_ITEMS = 3 * BATCH
 
@@ -283,24 +298,22 @@ def tile_mamba3mimoblock_pa_t_kernel(
 
         for item in range(AHEAD):
             prepare(-ROUND_ITEMS + LOG * BATCH + item)
-        copied = None
-        for phase in range(LOG - BATCH, GROUPS + FINISH_LAG):
+        copied = {}
+        steps = FIRST_STEP
+        for phase in range(LOG - BATCH, GROUPS):
             batch, kind = divmod(phase, BATCH)
-            finishing = phase - FINISH_LAG
             for q in range(BATCH):
                 g = batch * BATCH + q
+                sub_step = phase * BATCH + q
 
-                if q == 0 and 0 <= finishing:
-                    rotate_products(finishing)
-                if q == 1 and 0 <= finishing + 1 < GROUPS:
-                    damp(finishing + 1)
-                    turn_to_rows(finishing + 1)
-                if q == 2 and 0 <= finishing:
-                    rotate_sums(finishing)
+                if phase >= SINES:
+                    pace = QUICK if kind in (SINES, EXP_TANH) else SLOW
+                    for n in range(steps, steps + pace):
+                        finish_step(*divmod(n, FINISH_STEPS))
+                    steps += pace
 
-                if copied is not None:
-                    quantise_pass(*copied)
-                copied = None
+                if sub_step - QUANT_LAG in copied:
+                    quantise_pass(*copied[sub_step - QUANT_LAG])
                 if kind in (LOG, DECAY) and batch + 1 < BATCHES:
                     first = (batch + 1) * BATCH * GROUP_UNITS + ((kind - LOG) * BATCH + q) * STEP_UNITS
                     grouped = stage.tile([P, 4 * GROUP_ROWS], BF16, name="grouped", align_bytes=64)
@@ -310,11 +323,11 @@ def tile_mamba3mimoblock_pa_t_kernel(
                             grouped[:, h * 4 * UNIT : (h + 1) * 4 * UNIT],
                             on_vector=(batch < 1 and h == 0),
                         )
-                    copied = (grouped, first // GROUP_UNITS, first % GROUP_UNITS // STEP_UNITS)
+                    copied[sub_step] = (grouped, first // GROUP_UNITS, first % GROUP_UNITS // STEP_UNITS)
                     if kind == DECAY and q == 0:
                         load_state(batch + 1)
 
-                if 0 <= phase < GROUPS:
+                if 0 <= phase:
                     if kind == EXP_TANH:
                         exp_tanh(g)
                     if kind == LOG:
@@ -330,3 +343,6 @@ def tile_mamba3mimoblock_pa_t_kernel(
 
                 if kind != SINES:
                     prepare(batch * ROUND_ITEMS + kind * BATCH + q + AHEAD)
+
+        for n in range(steps, GROUPS * FINISH_STEPS):
+            finish_step(*divmod(n, FINISH_STEPS))

@@ -279,10 +279,10 @@ def tile_mamba3mimoblock_pa_t_kernel(
             if i == 4:
                 nc.vector.tensor_tensor(out=new_re, in0=new_re, in1=drive[:], op=ALU.add)
             if i == 6:
-                nc.gpsimd.tensor_tensor(out=new_im, in0=new_im, in1=im_cos, op=ALU.add)
+                nc.vector.tensor_tensor(out=new_im, in0=new_im, in1=im_cos, op=ALU.add)
                 nc.sync.dma_start(out=new_im_tiles[:, tiles, :], in_=new_im.rearrange("p (t c) -> p t c", c=CH))
             if i == 7:
-                nc.gpsimd.tensor_tensor(out=new_re, in0=new_re, in1=im_sin, op=ALU.subtract)
+                nc.vector.tensor_tensor(out=new_re, in0=new_re, in1=im_sin, op=ALU.subtract)
                 nc.sync.dma_start(out=new_re_tiles[:, tiles, :], in_=new_re.rearrange("p (t c) -> p t c", c=CH))
 
         ROUND_ITEMS = 3 * BATCH

@@ -192,7 +192,7 @@ def tile_mamba3mimoblock_pa_t_kernel(
         def wrap_angles(pair):
             turns = {}
             for g in pair:
-                turns[g] = chan.tile([P, GROUP_ROWS], F32, name="turns", bufs=2)
+                turns[g] = chan.tile([P, GROUP_ROWS], F32, name="turns", bufs=BATCH)
                 nc.vector.scalar_tensor_tensor(
                     out=angle[g][:], in0=step[g][:], scalar=half_turns[:], in1=angle[g][:], op0=ALU.mult, op1=ALU.add
                 )
@@ -205,7 +205,7 @@ def tile_mamba3mimoblock_pa_t_kernel(
                     out=turns[g][:], in0=turns[g][:], scalar1=ROUND_MAGIC, scalar2=2.0, op0=ALU.subtract, op1=ALU.mult
                 )
             for g in pair:
-                nc.vector.tensor_tensor(out=angle[g][:], in0=angle[g][:], in1=turns[g][:], op=ALU.subtract)
+                nc.gpsimd.tensor_tensor(out=angle[g][:], in0=angle[g][:], in1=turns[g][:], op=ALU.subtract)
 
         def exp_decay(g):
             decay[g] = chan.tile([P, GROUP_ROWS], F32, name="decay", bufs=IN_FLIGHT)
@@ -279,10 +279,10 @@ def tile_mamba3mimoblock_pa_t_kernel(
             if i == 4:
                 nc.vector.tensor_tensor(out=new_re, in0=new_re, in1=drive[:], op=ALU.add)
             if i == 6:
-                nc.vector.tensor_tensor(out=new_im, in0=new_im, in1=im_cos, op=ALU.add)
+                nc.gpsimd.tensor_tensor(out=new_im, in0=new_im, in1=im_cos, op=ALU.add)
                 nc.sync.dma_start(out=new_im_tiles[:, tiles, :], in_=new_im.rearrange("p (t c) -> p t c", c=CH))
             if i == 7:
-                nc.vector.tensor_tensor(out=new_re, in0=new_re, in1=im_sin, op=ALU.subtract)
+                nc.gpsimd.tensor_tensor(out=new_re, in0=new_re, in1=im_sin, op=ALU.subtract)
                 nc.sync.dma_start(out=new_re_tiles[:, tiles, :], in_=new_re.rearrange("p (t c) -> p t c", c=CH))
 
         ROUND_ITEMS = 3 * BATCH
@@ -321,7 +321,7 @@ def tile_mamba3mimoblock_pa_t_kernel(
                         copy_words(
                             unit_planes[first + h],
                             grouped[:, h * 4 * UNIT : (h + 1) * 4 * UNIT],
-                            on_vector=(batch < 1 and h == 0),
+                            on_vector=(h == 0 and (batch < 1 or kind == LOG)),
                         )
                     copied[sub_step] = (grouped, first // GROUP_UNITS, first % GROUP_UNITS // STEP_UNITS)
                     if kind == DECAY and q == 0:

import math
from contextlib import ExitStack

import concourse.mybir as mybir
from concourse.masks import make_identity

F32 = mybir.dt.float32
BF16 = mybir.dt.bfloat16
U32 = mybir.dt.uint32
U8 = mybir.dt.uint8
FP8X4 = mybir.dt.float8_e4m3fn_x4
ACT = mybir.ActivationFunctionType
ALU = mybir.AluOpType

P = 128
ROWS, K, CH = 8192, 1024, 128
FLOPS = 2 * ROWS * K * 3 * CH
TILES = ROWS // P
GROUP_TILES = 4
GROUP_ROWS = GROUP_TILES * P
GROUPS = TILES // GROUP_TILES
BATCH = 4
BATCHES = GROUPS // BATCH
PASSES = K // 512
ROW_WORDS = K // 2
UNIT = 256
GROUP_UNITS = PASSES * GROUP_ROWS // UNIT
STEP_UNITS = 2
EXP_TANH, LOG, DECAY, SINES = 0, 1, 2, 3
PREFETCH = 2
ROUND_MAGIC = 1.5 * 2.0**23
FEED_BANKS = 5
AHEAD = 2
QUANT_LAG = 2
FINISH_STEPS = 8
QUICK, SLOW = 3, 1
FIRST_STEP = (-2 * FINISH_STEPS + 5) - QUICK
IN_FLIGHT = BATCH + 3
WEIGHTS = ("dt", "ph", "b")


def tile_mamba3mimoblock_pa_t_kernel(
    tc, x, state_re, state_im, W_dt, b_dt, W_ph, b_ph, W_B, A_real, A_imag, out_0, out_1
):
    nc = tc.nc
    x_tiles = x.rearrange("(p t) k -> p t k", t=TILES)
    re_tiles = state_re.rearrange("(p t) c -> p t c", t=TILES)
    im_tiles = state_im.rearrange("(p t) c -> p t c", t=TILES)
    new_re_tiles = out_0.rearrange("(p t) c -> p t c", t=TILES)
    new_im_tiles = out_1.rearrange("(p t) c -> p t c", t=TILES)

    with ExitStack() as stack:
        stack.enter_context(tc.manual_schedule())
        const = stack.enter_context(tc.tile_pool(name="const", bufs=1))
        xin = stack.enter_context(tc.tile_pool(name="xin", bufs=PREFETCH + 1))
        stage = stack.enter_context(tc.tile_pool(name="stage", bufs=QUANT_LAG + 2))
        quant = stack.enter_context(tc.tile_pool(name="quant", bufs=3 * BATCH + 1))
        chan = stack.enter_context(tc.tile_pool(name="chan", bufs=BATCH))
        rows = stack.enter_context(tc.tile_pool(name="rows", bufs=3))
        psum = stack.enter_context(tc.psum_pool(name="psum", bufs=1))

        def transpose_words(word_blocks):
            planes = psum.tile([P, 2, UNIT], F32, name="planes", tag="feed", bufs=FEED_BANKS)
            for j, pair in enumerate(word_blocks):
                for u, words in enumerate(pair):
                    nc.tensor.transpose(planes[:, u, j * P : (j + 1) * P], words, ident[:])
            return planes

        def copy_words(planes, grouped_cols, on_vector):
            dst = grouped_cols.bitcast(F32).rearrange("p (r u) -> p r u", u=2)
            src = planes[:].rearrange("p u r -> p r u")
            if on_vector:
                nc.vector.tensor_copy(out=dst, in_=src)
            else:
                nc.scalar.copy(out=dst, in_=src)

        def quantise(grouped, codes_cols, scales_cols):
            nc.vector.quantize_mx(out=codes_cols.bitcast(FP8X4), scales=scales_cols, in_=grouped)

        vec_rows = const.tile([P, P], BF16, name="vec_rows")
        nc.vector.memset(vec_rows[:], 0.0)
        for j, vec in enumerate((b_dt, b_ph, A_real, A_imag)):
            nc.sync.dma_start(out=vec_rows[j : j + 1, :], in_=vec.rearrange("(o c) -> o c", o=1))
        w_raw = xin.tile([P, len(WEIGHTS) * K], BF16, name="w_raw", tag="x_raw")
        for i, w in enumerate((W_dt, W_ph, W_B)):
            nc.sync.dma_start(out=w_raw[:, i * K : (i + 1) * K], in_=w)

        x_raw = {}

        def load_x(g):
            x_raw[g] = xin.tile([P, GROUP_TILES * K], BF16, name="x_raw")
            nc.sync.dma_start(
                out=x_raw[g][:].rearrange("p (t k) -> p t k", t=GROUP_TILES),
                in_=x_tiles[:, g * GROUP_TILES : (g + 1) * GROUP_TILES, :],
            )

        for g in range(PREFETCH):
            load_x(g)

        re_all = const.tile([P, TILES * CH], BF16, name="re_all")
        im_all = const.tile([P, TILES * CH], BF16, name="im_all")

        def load_state(batch):
            t0, t1 = batch * BATCH * GROUP_TILES, (batch + 1) * BATCH * GROUP_TILES
            for dst, src in ((re_all, re_tiles), (im_all, im_tiles)):
                nc.sync.dma_start(
                    out=dst[:, t0 * CH : t1 * CH].rearrange("p (t c) -> p t c", c=CH), in_=src[:, t0:t1, :]
                )

        ident = const.tile([P, P], F32, name="ident")
        make_identity(nc, ident[:])

        vec_f32 = const.tile([P, P], F32, name="vec_f32")
        nc.vector.tensor_copy(out=vec_f32[:], in_=vec_rows[:])
        planes = psum.tile([P, 2, UNIT], F32, name="planes", tag="feed", bufs=FEED_BANKS)
        nc.tensor.transpose(planes[:, 0, 0:P], vec_f32[:], ident[:])
        per_channel = const.tile([P, 4], F32, name="per_channel")
        nc.vector.tensor_copy(out=per_channel[:], in_=planes[:, 0, 0:4])
        bias_dt, bias_ph = per_channel[:, 0:1], per_channel[:, 1:2]
        rate = const.tile([P, 1], F32, name="rate")
        nc.scalar.activation(out=rate[:], in_=per_channel[:, 2:3], func=ACT.Exp)
        neg_rate = const.tile([P, 1], F32, name="neg_rate")
        nc.vector.tensor_scalar(out=neg_rate[:], in0=rate[:], scalar1=-1.0, scalar2=None, op0=ALU.mult)
        half_turns = const.tile([P, 1], F32, name="half_turns")
        nc.vector.tensor_scalar(
            out=half_turns[:], in0=per_channel[:, 3:4], scalar1=1.0 / math.pi, scalar2=None, op0=ALU.mult
        )

        w_codes = const.tile([P, len(WEIGHTS) * UNIT], U32, name="w_codes", align_bytes=64)
        w_scales = const.tile([P, len(WEIGHTS) * UNIT], U8, name="w_scales", align_bytes=64)
        for i, name in enumerate(WEIGHTS):
            words = w_raw[:, i * K : (i + 1) * K].bitcast(F32)
            planes = transpose_words(
                [[words[:, (2 * c + u) * P : (2 * c + u + 1) * P] for u in range(2)] for c in range(PASSES)]
            )
            grouped = stage.tile([P, 4 * UNIT], BF16, name="w_grouped", tag="grouped", align_bytes=64)
            copy_words(planes, grouped[:], on_vector=True)
            quantise(grouped[:], w_codes[:, i * UNIT : (i + 1) * UNIT], w_scales[:, i * UNIT : (i + 1) * UNIT])

        def weight(name, c):
            lo = WEIGHTS.index(name) * UNIT + c * CH
            return w_codes[:, lo : lo + CH].bitcast(FP8X4), w_scales[:, lo : lo + CH]

        unit_planes, codes, scales = {}, {}, {}
        step, angle, decay, cos_sin = {}, {}, {}, {}
        turned, result, sums = {}, {}, {}

        def transpose_unit(k):
            g, in_group = divmod(k, GROUP_UNITS)
            c, h = divmod(in_group, GROUP_ROWS // UNIT)
            if in_group == 0 and g + PREFETCH < GROUPS:
                load_x(g + PREFETCH)
            words = x_raw[g][:].bitcast(F32)
            blocks = []
            for j in range(UNIT // P):
                lo = (h * (UNIT // P) + j) * ROW_WORDS + 2 * c * P
                blocks.append([words[:, lo + u * P : lo + (u + 1) * P] for u in range(2)])
            unit_planes[k] = transpose_words(blocks)

        def quantise_pass(grouped, g, c):
            if c == 0:
                codes[g] = quant.tile([P, PASSES * GROUP_ROWS], U32, name="codes", align_bytes=64)
                scales[g] = quant.tile([P, PASSES * GROUP_ROWS], U8, name="scales", align_bytes=64)
            cols = slice(c * GROUP_ROWS, (c + 1) * GROUP_ROWS)
            quantise(grouped[:], codes[g][:, cols], scales[g][:, cols])

        def multiply(g):
            sums[g] = {}
            for name in ("dt", "ph"):
                sums[g][name] = psum.tile([P, GROUP_ROWS], F32, name="sums_" + name, tag="feed", bufs=FEED_BANKS)
                for c in range(PASSES):
                    w_c, w_s = weight(name, c)
                    nc.tensor.matmul_mx(
                        out=sums[g][name][:],
                        lhsT=w_c,
                        lhsT_scale=w_s,
                        rhs=codes[g][:, c * GROUP_ROWS : (c + 1) * GROUP_ROWS].bitcast(FP8X4),
                        rhs_scale=scales[g][:, c * GROUP_ROWS : (c + 1) * GROUP_ROWS],
                        start=(c == 0),
                        stop=(c == PASSES - 1),
                    )

        def exp_tanh(g):
            step[g] = chan.tile([P, GROUP_ROWS], F32, name="step")
            angle[g] = chan.tile([P, GROUP_ROWS], F32, name="angle")
            nc.scalar.activation(out=step[g][:], in_=sums[g]["dt"][:], func=ACT.Exp, bias=bias_dt)
            nc.scalar.activation(out=angle[g][:], in_=sums[g]["ph"][:], func=ACT.Tanh, bias=bias_ph)

        def log(g):
            nc.scalar.activation(out=step[g][:], in_=step[g][:], func=ACT.Ln, bias=1.0)

        def wrap_angles(pair):
            turns = {}
            for g in pair:
                turns[g] = chan.tile([P, GROUP_ROWS], F32, name="turns", bufs=BATCH)
                nc.vector.scalar_tensor_tensor(
                    out=angle[g][:], in0=step[g][:], scalar=half_turns[:], in1=angle[g][:], op0=ALU.mult, op1=ALU.add
                )
            for g in pair:
                nc.vector.tensor_scalar(
                    out=turns[g][:], in0=angle[g][:], scalar1=0.5, scalar2=ROUND_MAGIC, op0=ALU.mult, op1=ALU.add
                )
            for g in pair:
                nc.vector.tensor_scalar(
                    out=turns[g][:], in0=turns[g][:], scalar1=ROUND_MAGIC, scalar2=2.0, op0=ALU.subtract, op1=ALU.mult
                )
            for g in pair:
                nc.gpsimd.tensor_tensor(out=angle[g][:], in0=angle[g][:], in1=turns[g][:], op=ALU.subtract)

        def exp_decay(g):
            decay[g] = chan.tile([P, GROUP_ROWS], F32, name="decay", bufs=IN_FLIGHT)
            nc.scalar.activation(out=decay[g][:], in_=step[g][:], func=ACT.Exp, scale=neg_rate[:])

        def sines(g):
            cos_sin[g] = chan.tile([P, 2, GROUP_ROWS], F32, name="cos_sin", bufs=IN_FLIGHT)
            nc.scalar.activation(out=cos_sin[g][:, 0, :], in_=angle[g][:], func=ACT.Abs)
            nc.scalar.activation(out=cos_sin[g][:, 1, :], in_=angle[g][:], func=ACT.Sin, scale=math.pi)
            nc.scalar.activation(
                out=cos_sin[g][:, 0, :], in_=cos_sin[g][:, 0, :], func=ACT.Sin, scale=-math.pi, bias=math.pi / 2
            )

        def damp(g):
            nc.vector.tensor_tensor(
                out=cos_sin[g][:],
                in0=cos_sin[g][:],
                in1=decay[g][:].unsqueeze(1).to_broadcast([P, 2, GROUP_ROWS]),
                op=ALU.mult,
            )

        def turn_to_rows(g):
            cos_t = psum.tile([P, GROUP_ROWS], F32, name="cos_t")
            sin_t = psum.tile([P, GROUP_ROWS], F32, name="sin_t")
            drive = psum.tile([P, GROUP_ROWS], F32, name="drive")
            for half, bank in enumerate((cos_t, sin_t)):
                for i in range(GROUP_TILES):
                    cols = slice(i * P, (i + 1) * P)
                    nc.tensor.transpose(bank[:, cols], cos_sin[g][:, half, cols], ident[:])
            for i in range(GROUP_TILES):
                for c in range(PASSES):
                    w_c, w_s = weight("b", c)
                    lo = c * GROUP_ROWS + i * P
                    nc.tensor.matmul_mx(
                        out=drive[:, i * P : (i + 1) * P],
                        lhsT=codes[g][:, lo : lo + P].bitcast(FP8X4),
                        lhsT_scale=scales[g][:, lo : lo + P],
                        rhs=w_c,
                        rhs_scale=w_s,
                        start=(c == 0),
                        stop=(c == PASSES - 1),
                    )
            turned[g] = (cos_t, sin_t, drive)

        def finish_step(g, i):
            if i == 5:
                if 0 <= g + 1 < GROUPS:
                    turn_to_rows(g + 1)
                if 0 <= g + 2 < GROUPS:
                    damp(g + 2)
            if g < 0 or i == 5:
                return
            if i == 0:
                result[g] = {}
                for name in ("new_re", "new_im", "im_sin", "im_cos"):
                    result[g][name] = rows.tile([P, GROUP_ROWS], F32, name=name)
            re = re_all[:, g * GROUP_ROWS : (g + 1) * GROUP_ROWS]
            im = im_all[:, g * GROUP_ROWS : (g + 1) * GROUP_ROWS]
            cos_t, sin_t, drive = turned[g]
            new_re, new_im = result[g]["new_re"][:], result[g]["new_im"][:]
            im_sin, im_cos = result[g]["im_sin"][:], result[g]["im_cos"][:]
            tiles = slice(g * GROUP_TILES, (g + 1) * GROUP_TILES)
            if i == 0:
                nc.vector.tensor_tensor(out=new_re, in0=re, in1=cos_t[:], op=ALU.mult)
            if i == 1:
                nc.vector.tensor_tensor(out=im_cos, in0=im, in1=cos_t[:], op=ALU.mult)
            if i == 2:
                nc.vector.tensor_tensor(out=new_im, in0=re, in1=sin_t[:], op=ALU.mult)
            if i == 3:
                nc.vector.tensor_tensor(out=im_sin, in0=im, in1=sin_t[:], op=ALU.mult)
            if i == 4:
                nc.vector.tensor_tensor(out=new_re, in0=new_re, in1=drive[:], op=ALU.add)
            if i == 6:
                nc.gpsimd.tensor_tensor(out=new_im, in0=new_im, in1=im_cos, op=ALU.add)
                nc.sync.dma_start(out=new_im_tiles[:, tiles, :], in_=new_im.rearrange("p (t c) -> p t c", c=CH))
            if i == 7:
                nc.gpsimd.tensor_tensor(out=new_re, in0=new_re, in1=im_sin, op=ALU.subtract)
                nc.sync.dma_start(out=new_re_tiles[:, tiles, :], in_=new_re.rearrange("p (t c) -> p t c", c=CH))

        ROUND_ITEMS = 3 * BATCH

        def prepare(item):
            batch, j = divmod(item, ROUND_ITEMS)
            if j < BATCH and 0 <= batch < BATCHES:
                multiply(batch * BATCH + j)
            if j >= BATCH and batch + 1 < BATCHES:
                first = (batch + 1) * BATCH * GROUP_UNITS + (j - BATCH) * STEP_UNITS
                for k in range(first, first + STEP_UNITS):
                    transpose_unit(k)

        for item in range(AHEAD):
            prepare(-ROUND_ITEMS + LOG * BATCH + item)
        copied = {}
        steps = FIRST_STEP
        for phase in range(LOG - BATCH, GROUPS):
            batch, kind = divmod(phase, BATCH)
            for q in range(BATCH):
                g = batch * BATCH + q
                sub_step = phase * BATCH + q

                if phase >= SINES:
                    pace = QUICK if kind in (SINES, EXP_TANH) else SLOW
                    for n in range(steps, steps + pace):
                        finish_step(*divmod(n, FINISH_STEPS))
                    steps += pace

                if sub_step - QUANT_LAG in copied:
                    quantise_pass(*copied[sub_step - QUANT_LAG])
                if kind in (LOG, DECAY) and batch + 1 < BATCHES:
                    first = (batch + 1) * BATCH * GROUP_UNITS + ((kind - LOG) * BATCH + q) * STEP_UNITS
                    grouped = stage.tile([P, 4 * GROUP_ROWS], BF16, name="grouped", align_bytes=64)
                    for h in range(STEP_UNITS):
                        copy_words(
                            unit_planes[first + h],
                            grouped[:, h * 4 * UNIT : (h + 1) * 4 * UNIT],
                            on_vector=(h == 0 and (batch < 1 or kind == LOG)),
                        )
                    copied[sub_step] = (grouped, first // GROUP_UNITS, first % GROUP_UNITS // STEP_UNITS)
                    if kind == DECAY and q == 0:
                        load_state(batch + 1)

                if 0 <= phase:
                    if kind == EXP_TANH:
                        exp_tanh(g)
                    if kind == LOG:
                        log(g)
                        if q == 2:
                            wrap_angles((g - 2, g - 1))
                    if kind == DECAY:
                        if q == 0:
                            wrap_angles((g + 2, g + 3))
                        exp_decay(g)
                    if kind == SINES:
                        sines(g)

                if kind != SINES:
                    prepare(batch * ROUND_ITEMS + kind * BATCH + q + AHEAD)

        for n in range(steps, GROUPS * FINISH_STEPS):
            finish_step(*divmod(n, FINISH_STEPS))
